import numpy as np
import ml_dtypes


def mxq(x, axis, fmt="e4m3"):
    dtype, down = {"e4m3": (ml_dtypes.float8_e4m3fn, 7), "e5m2": (ml_dtypes.float8_e5m2, 14)}[fmt]
    v = np.moveaxis(np.asarray(x, np.float32).astype(ml_dtypes.bfloat16).astype(np.float64), axis, -1)
    blocks = v.reshape(v.shape[:-1] + (-1, 32))
    amax = np.abs(blocks).max(-1, keepdims=True)
    byte = np.maximum(np.where(amax > 0, np.frexp(amax)[1] - 1 + 127, 0) - down, 1)
    scale = np.exp2(byte - 127.0)
    codes = (blocks / scale).astype(np.float32).astype(dtype).astype(np.float64)
    return np.moveaxis((codes * scale).reshape(v.shape), -1, axis)


WIDE = False


def mx_kscale(k):
    if not WIDE:
        return np.ones(k)
    levels = np.array([10, -10, 5, -5, 0])
    if k % 512:
        return np.exp2(np.random.permutation(np.resize(levels, k // 32))).repeat(32)
    a = np.empty((k // 512, 16))
    for p in range(k // 512):
        a[p, :8] = np.random.permutation(np.resize(levels, 8))
        for g in range(8):
            far = levels[np.abs(levels - a[p, g]) >= 10]
            a[p, g + 8] = far[np.random.randint(len(far))]
    return np.exp2(a.ravel()).repeat(32)


BF16 = ml_dtypes.bfloat16


def bf(x):
    return np.asarray(x, np.float32).astype(BF16)


def f64(x):
    return np.asarray(x).astype(np.float64)


B, S, D, M, R = 128, 16, 2048, 8, 1024
LN_EPS = 1e-5


def sigmoid(v):
    return 1.0 / (1.0 + np.exp(-v))


def layer_norm(x):
    mu = np.mean(x, axis=-1, keepdims=True)
    var = np.var(x, axis=-1, keepdims=True)
    return (x - mu) / np.sqrt(var + LN_EPS)


def draw0():
    s, t = mx_kscale(D), mx_kscale(R)
    return {"interface": bf(np.random.standard_normal((B, S, D)) * np.sqrt(S) * s),
            "memory": bf(0.5 + np.random.standard_normal((B, M, D))),
            "W_write_key": bf(np.random.standard_normal((R, D)) / np.sqrt(D) / s[None, :] * t[:, None]),
            "W_write_erase": bf(np.random.standard_normal((D, R)) * 1.5 / np.sqrt(R) / t[None, :]),
            "W_write_add": bf(np.random.standard_normal((D, R)) / np.sqrt(R) / t[None, :])}


def core(interface, memory, W_write_key, W_write_erase, W_write_add):
    i_mean = np.mean(f64(interface), axis=1)
    i_proj = mxq(i_mean, 1, "e4m3") @ mxq(f64(W_write_key), 1, "e4m3").T
    pq = mxq(i_proj, 1, "e4m3")
    erase = sigmoid(pq @ mxq(f64(W_write_erase), 1, "e4m3").T)[:, None, :]
    add = (pq @ mxq(f64(W_write_add), 1, "e4m3").T)[:, None, :]
    return layer_norm(f64(memory) * (1.0 - erase) + add)


def e4m3fn_bytes(y):
    return np.clip(np.asarray(y, np.float64), -448.0, 448.0).astype(np.float32).astype(ml_dtypes.float8_e4m3fn).view(np.uint8)


def e4m3fn_values(b):
    return np.asarray(b, np.uint8).view(ml_dtypes.float8_e4m3fn).astype(np.float64)


def setup_inputs():
    d = draw0()
    x0 = np.asarray(d['W_write_erase']).astype(np.float64)
    s = (np.max(np.abs(x0), axis=(0,), keepdims=True) / 448.0).astype(np.float32)
    out = {}
    for k, v in d.items():
        if k == 'W_write_erase':
            out['W_write_erase_bytes'] = e4m3fn_bytes(x0 / s.astype(np.float64))
            out['W_write_erase_scale'] = s
        else:
            out[k] = v
    return out


def reference(interface, memory, W_write_key, W_write_erase_bytes, W_write_erase_scale, W_write_add):
    return core(interface, memory, W_write_key, e4m3fn_values(W_write_erase_bytes) * W_write_erase_scale.astype(np.float64), W_write_add)

from contextlib import ExitStack

import concourse.mybir as mybir
from concourse.masks import make_identity

B, S, D, M, R = 128, 16, 2048, 8, 1024
FLOPS = 3 * 2 * B * D * R
BYTES = 2 * (B * S * D + B * M * D + 2 * R * D) + D * R + 4 * R + 4 * B * M * D

F32 = mybir.dt.float32
BF16 = mybir.dt.bfloat16
U32 = mybir.dt.uint32
U8 = mybir.dt.uint8
FP8 = mybir.dt.float8_e4m3fn
FP8X4 = mybir.dt.float8_e4m3fn_x4
ALU = mybir.AluOpType
ACT = mybir.ActivationFunctionType
AX = mybir.AxisListType
P = 128
EPS = 1e-5

K_RATE = 2
E_EARLY = 4
LOAD_ORDER = (0, 1, 2, 4, 3, 5, 6, 7)
G_MULT = (1, 3, 5, 7)
STEPS = "v0 A1 Q0 g x1 v2 A2 Q1 x3 A3 Q2 Q3 P a0 s0 v4 x5 a1 nv0 s1 ng1 x7 a2 s2 v6 a3 s3 ng2 a4 s4 ng3 a5 s5 ng4 a6 s6 ng5 a7 s7 nv6 ne7"


def tile_ultralightweightmemory_pa_kernel(
    tc, interface, memory, w_key, w_erase_bytes, w_erase_scale, w_add, out
):
    nc = tc.nc
    face_v = interface.rearrange("(J b) s d -> (b s) J d", J=16)
    key_v = w_key.rearrange("(h m t) k -> h m t k", h=2, t=4)
    add_v = w_add.rearrange("(c i j) k -> c i j k", c=4, j=4)
    byt_v = w_erase_bytes.rearrange("(c i j) k -> c i j k", c=4, j=4)

    with ExitStack() as ctx:
        keep = ctx.enter_context(tc.tile_pool(name="keep", bufs=1))
        io = ctx.enter_context(tc.tile_pool(name="io", bufs=11))
        wide_pool = ctx.enter_context(tc.tile_pool(name="wide", bufs=3))
        grp_pool = ctx.enter_context(tc.tile_pool(name="grp", bufs=4))
        small = ctx.enter_context(tc.tile_pool(name="small", bufs=8))
        psum_tr = ctx.enter_context(tc.psum_pool(name="psum_tr", bufs=4))
        psum_acc = ctx.enter_context(tc.psum_pool(name="psum_acc", bufs=4))

        ident = keep.tile([P, P], F32, name="ident")
        make_identity(nc, ident[:])
        ctx.enter_context(tc.manual_schedule())

        sel_f = keep.tile([P, 8], F32, name="sel_f")
        sel = keep.tile([P, 8], BF16, name="sel")
        dummy = keep.tile([P, 1], F32, name="dummy")
        scale_bc = keep.tile([P, R], F32, name="scale_bc")

        nc.sync.dma_start(out=scale_bc[:], in_=w_erase_scale.rearrange("o k -> (o k)").partition_broadcast(P))
        byte_tiles, key_raw, faces, add_raw, mems = [], [], [], [], []

        def load_bytes(c):
            byte_tile = keep.tile([P, 4, R], U8, name="byte_tile%d" % c)
            nc.sync.dma_start(out=byte_tile[:], in_=byt_v[c])
            byte_tiles.append(byte_tile)

        for c in range(4):
            if c < E_EARLY:
                load_bytes(c)
            raw = io.tile([P, 4, 1024], BF16, tag="io", name="key_raw")
            nc.sync.dma_start(out=raw[:], in_=key_v[c // 2][:, :, 1024 * (c % 2) : 1024 * (c % 2 + 1)])
            key_raw.append(raw)

        def load_face(n):
            face = io.tile([P, 2, D], BF16, tag="io", name="face")
            nc.sync.dma_start(out=face[:], in_=face_v[:, 2 * n : 2 * n + 2, :])
            faces.append(face)

        def load_add(c):
            raw = io.tile([P, 4, R], BF16, tag="io", name="add_raw")
            nc.sync.dma_start(out=raw[:], in_=add_v[c])
            add_raw.append(raw)

        def load_mems(n):
            pair = io.tile([P, 2, D], BF16, tag="io", name="pair")
            for i in range(2):
                nc.sync.dma_start(out=pair[:, i, :], in_=memory[:, 2 * n + i, :])
                mems.append(pair[:, i, :])

        for n in range(7):
            load_face(n)

        nc.vector.tensor_reduce(
            out=sel_f[:], in_=ident[:].rearrange("p (n s) -> p n s", s=S), axis=AX.X, op=ALU.add
        )
        nc.vector.tensor_scalar_mul(out=sel[:], in0=sel_f[:], scalar1=1.0 / S)
        nc.vector.memset(dummy[:], 0.0)
        nc.scalar.activation(out=dummy[:], in_=dummy[:], func=ACT.Sigmoid)

        def turn(words, pool, tag):
            bank = pool.tile([P, 2, 2, P], F32, tag=tag, name="bank")
            for g in range(2):
                for u in range(2):
                    nc.tensor.transpose(bank[:, g, u, :], words[:, 256 * g + u : 256 * (g + 1) : 2], ident[:])
            return bank

        def empty(bank, grp, j, copy):
            view = grp[:].rearrange("p g c t -> p (g c t)").bitcast(F32)
            view = view.rearrange("p (g c u) -> p g c u", g=2, u=2)
            copy(out=view[:, :, P * j : P * (j + 1), :], in_=bank[:].rearrange("p g u r -> p g r u"))

        def new_grp():
            grp = grp_pool.tile([P, 2, 512, 4], BF16, tag="grp", align_bytes=64, name="grp")
            return grp

        def quantize(grp, name):
            codes = keep.tile([P, 2, 512], U32, align_bytes=64, name=name + "_codes")
            planes = keep.tile([P, 2, 512], U8, align_bytes=64, name=name + "_planes")
            nc.vector.quantize_mx(
                out=codes[:].rearrange("p g c -> p (g c)").bitcast(FP8X4),
                scales=planes[:].rearrange("p g c -> p (g c)"),
                in_=grp[:].rearrange("p g c t -> p (g c t)"),
            )
            return codes, planes

        acc = []
        for g in range(4):
            bank = psum_acc.tile([P, 4, P], F32, tag="acc", name="mean_bank")
            acc.append(bank)

        def mean(J):
            face = faces[J // 2]
            for g in range(4):
                for t in range(4):
                    nc.tensor.matmul(
                        acc[g][:, t, 8 * J : 8 * J + 8],
                        lhsT=face[:, J % 2, 512 * g + t : 512 * (g + 1) : 4],
                        rhs=sel[:],
                        start=True,
                        stop=True,
                    )

        erase_q, key_q, add_q = [], [], []
        e_grps, k_grps = [], []
        e_wides = []

        def widen(n):
            wide = wide_pool.tile([P, R], BF16, tag="wide", name="wide")
            nc.vector.tensor_tensor(
                out=wide[:], in0=byte_tiles[n // 4][:, n % 4, :].bitcast(FP8), in1=scale_bc[:], op=ALU.mult
            )
            e_wides.append(wide)

        def unit_part(grps, n, words):
            if n % 4 == 0:
                grps.append(new_grp())
            bank = turn(words, psum_tr, "tr")
            empty(bank, grps[n // 4], n % 4, nc.scalar.copy)

        k_done, j_done = 0, 0
        for n in range(4 * E_EARLY):
            widen(n)
            if n in (4, 6, 8, 11):
                x = len(key_q)
                key_q.append(quantize(k_grps[x], "key%d" % x))
            if n in (5, 10, 14):
                x = len(erase_q)
                erase_q.append(quantize(e_grps[x], "erase%d" % x))
            k_goal = min(16, K_RATE * n)
            half = (k_done + k_goal) // 2
            while k_done < half:
                unit_part(k_grps, k_done, key_raw[k_done // 4][:, k_done % 4, :].bitcast(F32))
                k_done += 1
            unit_part(e_grps, n, e_wides[n][:].bitcast(F32))
            while k_done < k_goal:
                unit_part(k_grps, k_done, key_raw[k_done // 4][:, k_done % 4, :].bitcast(F32))
                k_done += 1
            j_goal = max(0, 3 * (n - 8) // 2)
            while j_done < j_goal:
                mean(j_done)
                j_done += 1
            if n == 8:
                load_face(7)
        for c in range(E_EARLY, 4):
            load_bytes(c)
        for item in LOAD_ORDER:
            if item < 4:
                load_add(item)
            else:
                load_mems(item - 4)

        while j_done < 14:
            mean(j_done)
            j_done += 1
        if E_EARLY == 4:
            erase_q.append(quantize(e_grps[3], "erase3"))
        im_grp = keep.tile([P, 4, P, 4], BF16, align_bytes=64, name="im_grp")
        im_codes = keep.tile([P, 4, P], U32, align_bytes=64, name="im_codes")
        im_planes = keep.tile([P, 4, P], U8, align_bytes=64, name="im_planes")

        def mean_out(g, b0, b1, copy):
            copy(out=im_grp[:, g, b0:b1, :], in_=acc[g][:, :, b0:b1].rearrange("p t b -> p b t"))

        for g in range(4):
            mean_out(g, 0, 112, nc.scalar.copy if g % 2 else nc.vector.tensor_copy)
        mean(14)
        mean(15)
        for g in range(4):
            mean_out(g, 112, 128, nc.scalar.copy if g % 2 else nc.vector.tensor_copy)
        for x in range(2):
            nc.vector.quantize_mx(
                out=im_codes[:, 2 * x : 2 * x + 2, :].rearrange("p g b -> p (g b)").bitcast(FP8X4),
                scales=im_planes[:, 2 * x : 2 * x + 2, :].rearrange("p g b -> p (g b)"),
                in_=im_grp[:, 2 * x : 2 * x + 2, :, :].rearrange("p g b t -> p (g b t)"),
            )

        a_grps = []

        def add_part(c, j, copy):
            if j == 0:
                a_grps.append(new_grp())
            bank = turn(add_raw[c][:, j, :].bitcast(F32), psum_acc, "acc")
            empty(bank, a_grps[c], j, copy)

        def add_quantize(c):
            add_q.append(quantize(a_grps[c], "add%d" % c))

        pq_grp = keep.tile([P, 2, P, 4], BF16, align_bytes=64, name="pq_grp")
        pq_codes = keep.tile([P, 2, P], U32, align_bytes=64, name="pq_codes")
        pq_planes = keep.tile([P, 2, P], U8, align_bytes=64, name="pq_planes")
        for h in range(2):
            bank = psum_acc.tile([P, 4, P], F32, tag="acc", name="proj_bank")
            for t in range(4):
                for g in range(4):
                    codes, planes = key_q[2 * h + g // 2]
                    cols = slice(P * t, P * (t + 1))
                    nc.tensor.matmul_mx(
                        out=bank[:, t, :],
                        lhsT=codes[:, g % 2, cols].bitcast(FP8X4),
                        lhsT_scale=planes[:, g % 2, cols],
                        rhs=im_codes[:, g, :].bitcast(FP8X4),
                        rhs_scale=im_planes[:, g, :],
                        start=(g == 0),
                        stop=(g == 3),
                    )
            copy = nc.scalar.copy if h == 0 else nc.vector.tensor_copy
            copy(out=pq_grp[:, h, :, :], in_=bank[:].rearrange("p t b -> p b t"))
            nc.vector.quantize_mx(
                out=pq_codes[:, h, :].bitcast(FP8X4),
                scales=pq_planes[:, h, :],
                in_=pq_grp[:, h, :, :].rearrange("p b t -> p (b t)"),
            )
        for j in range(2):
            add_part(0, j, nc.vector.tensor_copy)

        gate_t = io.tile([P, 4, 4, P], F32, tag="io", name="gate_t")
        gate_sb = keep.tile([P, D], F32, name="gate_sb")
        erase_banks, gates = [], []
        for c in range(4):
            bank = psum_tr.tile([P, 4, P], F32, tag="tr", name="erase_bank")
            erase_banks.append(bank)
        for c in range(4):
            bank = psum_tr.tile([P, 4, P], F32, tag="tr", name="gate_bank")
            gates.append(bank)

        def erase_product(c):
            codes, planes = erase_q[c]
            for j in range(4):
                cols = slice(P * j, P * (j + 1))
                for h in range(2):
                    nc.tensor.matmul_mx(
                        out=erase_banks[c][:, j, :],
                        lhsT=codes[:, h, cols].bitcast(FP8X4),
                        lhsT_scale=planes[:, h, cols],
                        rhs=pq_codes[:, h, :].bitcast(FP8X4),
                        rhs_scale=pq_planes[:, h, :],
                        start=(h == 0),
                        stop=(h == 1),
                    )
            nc.scalar.activation(out=gate_t[:, c, :, :], in_=erase_banks[c][:], func=ACT.Sigmoid, scale=-1.0)

        def gate_turn(c):
            for j in range(4):
                nc.tensor.transpose(gates[c][:, j, :], gate_t[:, c, j, :], ident[:])

        def gate_copy(c):
            nc.scalar.copy(
                out=gate_sb[:, 512 * c : 512 * (c + 1)].rearrange("p (i j) -> p i j", j=4),
                in_=gates[c][:].rearrange("p j i -> p i j"),
            )

        erase_product(0)
        erase_product(1)
        erase_product(2)
        gate_turn(0)
        erase_product(3)
        gate_turn(1)
        gate_turn(2)
        gate_turn(3)
        for j in range(2, 4):
            add_part(0, j, nc.scalar.copy)

        xs = []
        for m in range(8):
            xs.append(None)

        def mult(m):
            x = io.tile([P, D], F32, tag="io", name="x")
            xs[m] = x
            for c in range(4):
                cols = slice(512 * c, 512 * (c + 1))
                if m in G_MULT:
                    nc.gpsimd.tensor_tensor(out=x[:, cols], in0=mems[m][:, cols], in1=gate_sb[:, cols], op=ALU.mult)
                else:
                    nc.vector.tensor_tensor(
                        out=x[:, cols].rearrange("p (i j) -> p i j", j=4),
                        in0=mems[m][:, cols].rearrange("p (i j) -> p i j", j=4),
                        in1=gates[c][:].rearrange("p j i -> p i j"),
                        op=ALU.mult,
                    )

        add_banks = []

        def add_products():
            for c in range(4):
                bank = psum_acc.tile([P, 512], F32, tag="acc", name="add_bank")
                codes, planes = add_q[c]
                for h in range(2):
                    nc.tensor.matmul_mx(
                        out=bank[:],
                        lhsT=pq_codes[:, h, :].bitcast(FP8X4),
                        lhsT_scale=pq_planes[:, h, :],
                        rhs=codes[:, h, :].bitcast(FP8X4),
                        rhs_scale=planes[:, h, :],
                        start=(h == 0),
                        stop=(h == 1),
                    )
                add_banks.append(bank)

        sums = {}

        def add(m):
            part = small.tile([P, 4], F32, tag="part", name="part")
            sums[m] = part
            for c in range(4):
                x_view = xs[m][:, 512 * c : 512 * (c + 1)].rearrange("p (i j) -> p i j", j=4)
                nc.vector.scalar_tensor_tensor(
                    out=x_view,
                    in0=x_view,
                    scalar=1.0,
                    in1=add_banks[c][:].rearrange("p (j i) -> p i j", j=4),
                    op0=ALU.mult,
                    op1=ALU.add,
                    accum_out=part[:, c : c + 1],
                )

        neg_mu, rstd, shift = {}, {}, {}
        junk = im_grp[:].rearrange("p g b t -> p (g b t)")

        def stats(m):
            tiny = small.tile([P, 4], F32, tag="tiny", name="tiny")
            mean_m = small.tile([P, 1], F32, tag="mean_m", name="mean_m")
            nc.scalar.activation(out=tiny[:], in_=sums[m][:], func=ACT.Copy, scale=-1.0 / D, accum_out=mean_m[:])
            square = small.tile([P, 1], F32, tag="square", name="square")
            nc.scalar.activation(out=junk, in_=xs[m][:], func=ACT.Square, bias=mean_m[:], accum_out=square[:])
            rstd_m = small.tile([P, 1], F32, tag="rstd_m", name="rstd_m")
            nc.scalar.activation(out=rstd_m[:], in_=square[:], func=ACT.Abs_reciprocal_sqrt, scale=1.0 / D, bias=EPS)
            neg_mu[m], rstd[m] = mean_m, rstd_m

        def norm_s(m, cols):
            low = small.tile([P, 1], F32, tag="shift", name="low")
            nc.scalar.activation(out=low[:], in_=neg_mu[m][:], func=ACT.Copy, scale=rstd[m][:])
            nc.scalar.activation(
                out=xs[m][:, cols], in_=xs[m][:, cols], func=ACT.Identity, scale=rstd[m][:], bias=low[:]
            )

        def norm_ts(m, cols, engine):
            engine.tensor_scalar(
                out=xs[m][:, cols], in0=xs[m][:, cols], scalar1=neg_mu[m][:], scalar2=rstd[m][:], op0=ALU.add, op1=ALU.mult
            )

        def store(m, cols):
            nc.sync.dma_start(out=out[:, m, cols], in_=xs[m][:, cols])

        everything = slice(0, D)
        for step in STEPS.split(" "):
            m = int(step[-1]) if len(step) > 1 else 0
            kind = step[:-1] if len(step) > 1 else step
            if kind == "v" or kind == "x":
                mult(m)
            elif kind == "A":
                for j in range(4):
                    add_part(m, j, nc.scalar.copy)
            elif kind == "Q":
                add_quantize(m)
            elif kind == "g":
                for c in range(4):
                    gate_copy(c)
            elif kind == "P":
                nc.scalar.activation(out=dummy[:], in_=dummy[:], func=ACT.Abs_reciprocal_sqrt)
                add_products()
            elif kind == "a":
                add(m)
            elif kind == "s":
                stats(m)
            elif kind == "ns":
                norm_s(m, everything)
                store(m, everything)
            elif kind == "nv":
                norm_ts(m, everything, nc.vector)
                store(m, everything)
            elif kind == "ng":
                for i in range(2):
                    cols = slice(1024 * i, 1024 * (i + 1))
                    norm_ts(m, cols, nc.gpsimd)
                store(m, everything)
            elif kind == "ne":
                norm_ts(m, slice(0, 1280), nc.vector)
                store(m, slice(0, 1280))
                norm_s(m, slice(1280, D))
                store(m, slice(1280, D))
